import numpy as np
import ml_dtypes


def mxq(x, axis, fmt="e4m3"):
    dtype, down = {"e4m3": (ml_dtypes.float8_e4m3fn, 7), "e5m2": (ml_dtypes.float8_e5m2, 14)}[fmt]
    v = np.moveaxis(np.asarray(x, np.float32).astype(ml_dtypes.bfloat16).astype(np.float64), axis, -1)
    blocks = v.reshape(v.shape[:-1] + (-1, 32))
    amax = np.abs(blocks).max(-1, keepdims=True)
    byte = np.maximum(np.where(amax > 0, np.frexp(amax)[1] - 1 + 127, 0) - down, 1)
    scale = np.exp2(byte - 127.0)
    codes = (blocks / scale).astype(np.float32).astype(dtype).astype(np.float64)
    return np.moveaxis((codes * scale).reshape(v.shape), -1, axis)


WIDE = False


def mx_kscale(k):
    if not WIDE:
        return np.ones(k)
    levels = np.array([10, -10, 5, -5, 0])
    a = np.random.permutation(np.resize(levels, k // 512 * 4)).reshape(k // 512, 4)
    idx = np.arange(k)
    return np.exp2(a[idx // 512, idx % 128 // 32])


BF16 = ml_dtypes.bfloat16


def bf(x):
    return np.asarray(x, np.float32).astype(BF16)


def f64(x):
    return np.asarray(x).astype(np.float64)


B, H, W, C, NS = 2, 2, 4096, 128, 8
WIN = W // NS
SHIFT = WIN // 2


def setup_inputs():
    s = mx_kscale(WIN)
    sv = np.roll(np.tile(s.max() / s, NS), SHIFT)
    return {"q": bf(np.random.standard_normal((B, H * W, C))),
            "k": bf(np.random.standard_normal((B, H * W, C))),
            "v": bf((np.random.standard_normal((B, H, W, C)) * 2.0 * sv[None, None, :, None]).reshape(B, H * W, C)),
            "attn_mask": bf(np.random.standard_normal((NS, WIN, WIN)) + np.log(s)[None, None, :]),
            "h": H, "w": W, "num_splits": NS}


def reference(q, k, v, attn_mask, h, w, num_splits):
    b, hw, c = q.shape
    assert hw == h * w
    win = w // num_splits
    shift = win // 2
    scale = c ** 0.5

    def prep(x):
        x = f64(x).reshape(b * h, w, c)
        x = np.roll(x, -shift, axis=1)
        return x.reshape(b * h, num_splits, win, c)

    qs, ks, vs = prep(q), prep(k), prep(v)
    scores = qs @ ks.transpose(0, 1, 3, 2) / scale
    scores = scores + f64(attn_mask)[None]
    e = np.exp(scores - scores.max(-1, keepdims=True))
    out = (mxq(e, 3, "e4m3") @ mxq(vs, 2, "e4m3")) / e.sum(-1, keepdims=True)
    out = out.reshape(b, h, w, c)
    out = np.roll(out, shift, axis=2)
    return out.reshape(b, h * w, c)

@@ -1,0 +1,272 @@
+import math
+from contextlib import ExitStack
+
+import concourse.bass as bass
+import concourse.mybir as mybir
+import concourse.tile as tile
+from concourse.masks import make_identity
+
+F32 = mybir.dt.float32
+BF16 = mybir.dt.bfloat16
+U32 = mybir.dt.uint32
+U8 = mybir.dt.uint8
+FP8X4 = mybir.dt.float8_e4m3fn_x4
+ALU = mybir.AluOpType
+ACT = mybir.ActivationFunctionType
+AX = mybir.AxisListType
+
+P = 128
+C = 128
+ROWS = 4
+WPR = 8
+WIN = 512
+TPR = 32
+NWIN = ROWS * WPR
+NG = NWIN * 4
+NCH = NWIN // 2
+SCALE = 1.0 / math.sqrt(128.0)
+FLOPS = 2 * NWIN * 2 * WIN * WIN * C
+
+
+def tile_single_head_split_window_attention_1d_t_kernel(tc, q, k, v, attn_mask, h, w, num_splits, out):
+    nc = tc.nc
+    qv = q.flatten_outer_dims().rearrange("(r t p) c -> r p t c", t=TPR, p=P)
+    kv = k.flatten_outer_dims().rearrange("(r t p) c -> r p t c", t=TPR, p=P)
+    vv = v.flatten_outer_dims().rearrange("(r t p) c -> r p t c", t=TPR, p=P)
+    ov = out.flatten_outer_dims().rearrange("(r t p) c -> r p t c", t=TPR, p=P)
+
+    with ExitStack() as ctx:
+        const = ctx.enter_context(tc.tile_pool(name="const", bufs=1))
+        raw = ctx.enter_context(tc.tile_pool(name="raw", bufs=4))
+        work = ctx.enter_context(tc.tile_pool(name="work", bufs=3))
+        small = ctx.enter_context(tc.tile_pool(name="small", bufs=8))
+        ps_s = ctx.enter_context(tc.psum_pool(name="ps_s", bufs=3))
+        ps_e = ctx.enter_context(tc.psum_pool(name="ps_e", bufs=2))
+        ps_o = ctx.enter_context(tc.psum_pool(name="ps_o", bufs=2))
+        ps_t = ctx.enter_context(tc.psum_pool(name="ps_t", bufs=1))
+
+        ident = const.tile([P, P], BF16, name="ident")
+        make_identity(nc, ident[:])
+        bias = const.tile([P, WPR, 4, WIN], BF16, name="bias")
+
+        st = {}
+
+        def load_rows(dst, src, row, ch_in_row):
+            t0 = 2 + 8 * ch_in_row
+            if t0 + 8 <= TPR:
+                nc.sync.dma_start(out=dst[:, :, :], in_=src[row, :, t0:t0 + 8, :])
+            else:
+                nc.sync.dma_start(out=dst[:, 0:6, :], in_=src[row, :, t0:TPR, :])
+                nc.sync.dma_start(out=dst[:, 6:8, :], in_=src[row, :, 0:2, :])
+
+        def load_bias(n):
+            nc.sync.dma_start(out=bias[:, n, :, :], in_=attn_mask[n].rearrange("(j p) x -> p j x", p=P))
+
+        def load_chunk(ch):
+            if ch >= NCH:
+                return
+            row, cr = ch // 4, ch % 4
+            q_raw = raw.tile([P, 8, C], BF16, tag="q_raw")
+            k_raw = raw.tile([P, 8, C], BF16, tag="k_raw")
+            v_raw = raw.tile([P, 8, C], BF16, tag="v_raw")
+            load_rows(q_raw, qv, row, cr)
+            load_rows(k_raw, kv, row, cr)
+            if row == 0:
+                load_bias(2 * cr)
+            load_rows(v_raw, vv, row, cr)
+            if row == 0:
+                load_bias(2 * cr + 1)
+            st[("q", ch)] = q_raw
+            st[("k", ch)] = k_raw
+            st[("v", ch)] = v_raw
+
+        def vprep(ch):
+            if ch >= NCH:
+                return
+            v_raw = st[("v", ch)]
+            vg = work.tile([P, 2, C, 4], BF16, tag="vg", align_bytes=64)
+            for a in range(2):
+                nc.vector.tensor_copy(
+                    out=vg[:, a, :, :],
+                    in_=v_raw[:, 4 * a:4 * a + 4, :].rearrange("p t c -> p c t"),
+                )
+            vc = work.tile([P, 2 * C], U32, tag="vc", align_bytes=64)
+            vs = work.tile([P, 2 * C], U8, tag="vs", align_bytes=64)
+            nc.vector.quantize_mx(
+                out=vc[:].bitcast(FP8X4),
+                scales=vs[:],
+                in_=vg[:].rearrange("p a c t -> p (a c t)"),
+            )
+            st[("vc", ch)] = vc
+            st[("vs", ch)] = vs
+
+        def tr_qk(wi):
+            if wi >= NWIN:
+                return
+            ch, a = wi // 2, wi % 2
+            q_raw = st[("q", ch)]
+            k_raw = st[("k", ch)]
+            tp = ps_t.tile([P, 8, P], BF16, tag="tp")
+            for j in range(4):
+                nc.tensor.transpose(tp[:, j, :], q_raw[:, 4 * a + j, :], ident[:])
+            for j in range(4):
+                nc.tensor.transpose(tp[:, 4 + j, :], k_raw[:, 4 * a + j, :], ident[:])
+            qkT = work.tile([P, 8, P], BF16, tag="qkT")
+            nc.scalar.copy(out=qkT[:], in_=tp[:])
+            st[("qkT", wi)] = qkT
+
+        def qk(g):
+            if g < 0 or g >= NG:
+                return
+            wi, j = g // 4, g % 4
+            qkT = st[("qkT", wi)]
+            s_ps = ps_s.tile([P, WIN], F32, tag="s_ps")
+            nc.tensor.matmul(
+                s_ps[:],
+                lhsT=qkT[:, j, :],
+                rhs=qkT[:, 4:8, :].rearrange("c t x -> c (t x)"),
+                start=True,
+                stop=True,
+            )
+            st[("s_ps", g)] = s_ps
+
+        def bias_max(g):
+            if g < 0 or g >= NG:
+                return
+            wi, j = g // 4, g % 4
+            s_ps = st[("s_ps", g)]
+            ns = work.tile([P, WIN], F32, tag="ns", bufs=4)
+            nc.vector.scalar_tensor_tensor(
+                out=ns[:], in0=s_ps[:], scalar=-SCALE, in1=bias[:, wi % WPR, j, :],
+                op0=ALU.mult, op1=ALU.subtract,
+            )
+            nm = small.tile([P, 1], F32, tag="nm")
+            nc.vector.tensor_reduce(out=nm[:], in_=ns[:], axis=AX.X, op=ALU.min)
+            st[("ns", g)] = ns
+            st[("nm", g)] = nm
+
+        def expo(g):
+            if g < 0 or g >= NG:
+                return
+            wi, j = g // 4, g % 4
+            if j == 0:
+                rs_new = small.tile([P, 4], F32, tag="rs")
+                st[("rs", wi)] = rs_new
+            rs = st[("rs", wi)]
+            ns = st[("ns", g)]
+            nm = st[("nm", g)]
+            e = work.tile([P, WIN], BF16, tag="e", bufs=4)
+            nc.scalar.activation(
+                out=e[:], in_=ns[:], func=ACT.Exp, bias=nm[:, 0:1], scale=-1.0,
+                accum_out=rs[:, j:j + 1],
+            )
+            st[("e", g)] = e
+
+        def tr_e(g):
+            if g < 0 or g >= NG:
+                return
+            pr, a = g // 2, g % 2
+            if a == 0:
+                et_new = ps_e.tile([P, 2, 4, P], BF16, tag="et")
+                st[("et", pr)] = et_new
+            et = st[("et", pr)]
+            e = st[("e", g)]
+            for t in range(4):
+                nc.tensor.transpose(et[:, a, t, :], e[:, t * P:(t + 1) * P], ident[:])
+
+        def evict_e(pr):
+            if pr < 0 or pr >= NG // 2:
+                return
+            wi, hh = pr // 2, pr % 2
+            if hh == 0:
+                grp_new = work.tile([P, WIN, 4], BF16, tag="grp", align_bytes=64)
+                st[("grp", wi)] = grp_new
+            grp = st[("grp", wi)]
+            et = st[("et", pr)]
+            nc.scalar.copy(
+                out=grp[:, 256 * hh:256 * (hh + 1), :].rearrange("p (a x) t -> p a x t", a=2),
+                in_=et[:].rearrange("p a t x -> p a x t"),
+            )
+
+        def quant(wi):
+            if wi < 0 or wi >= NWIN:
+                return
+            grp = st[("grp", wi)]
+            ec = work.tile([P, WIN], U32, tag="ec", align_bytes=64)
+            es = work.tile([P, WIN], U8, tag="es", align_bytes=64)
+            nc.vector.quantize_mx(
+                out=ec[:].bitcast(FP8X4), scales=es[:], in_=grp[:].rearrange("p x t -> p (x t)"),
+            )
+            st[("ec", wi)] = ec
+            st[("es", wi)] = es
+
+        def mx(wi):
+            if wi < 0 or wi >= NWIN:
+                return
+            ch, a = wi // 2, wi % 2
+            ec = st[("ec", wi)]
+            es = st[("es", wi)]
+            vc = st[("vc", ch)]
+            vs = st[("vs", ch)]
+            o_ps = ps_o.tile([P, 4, C], F32, tag="o_ps")
+            for j in range(4):
+                nc.tensor.matmul_mx(
+                    out=o_ps[:, j, :],
+                    lhsT=ec[:, j * P:(j + 1) * P].bitcast(FP8X4),
+                    lhsT_scale=es[:, j * P:(j + 1) * P],
+                    rhs=vc[:, a * C:(a + 1) * C].bitcast(FP8X4),
+                    rhs_scale=vs[:, a * C:(a + 1) * C],
+                    start=True,
+                    stop=True,
+                )
+            st[("o_ps", wi)] = o_ps
+
+        def finish(wi):
+            if wi < 0 or wi >= NWIN:
+                return
+            row, n = wi // WPR, wi % WPR
+            o_ps = st[("o_ps", wi)]
+            rs = st[("rs", wi)]
+            ri = small.tile([P, 4], F32, tag="ri")
+            nc.vector.reciprocal(out=ri[:], in_=rs[:])
+            o_sb = work.tile([P, 4, C], F32, tag="o_sb")
+            if wi % 2 == 0:
+                nc.vector.tensor_tensor(
+                    out=o_sb[:], in0=o_ps[:], in1=ri[:].unsqueeze(2).to_broadcast([P, 4, C]), op=ALU.mult,
+                )
+            else:
+                for j in range(4):
+                    nc.scalar.activation(out=o_sb[:, j, :], in_=o_ps[:, j, :], func=ACT.Copy, scale=ri[:, j:j + 1])
+            t0 = 2 + 4 * n
+            if t0 + 4 <= TPR:
+                nc.sync.dma_start(out=ov[row, :, t0:t0 + 4, :], in_=o_sb[:])
+            else:
+                nc.sync.dma_start(out=ov[row, :, t0:TPR, :], in_=o_sb[:, 0:2, :])
+                nc.sync.dma_start(out=ov[row, :, 0:2, :], in_=o_sb[:, 2:4, :])
+
+        load_chunk(0)
+        load_chunk(1)
+        load_chunk(2)
+        tr_qk(0)
+        for g in range(-2, NG + 10):
+            wi, j = g // 4, g % 4
+            if g >= 0 and g % 8 == 0:
+                load_chunk(g // 8 + 3)
+            if j == 0 and g >= 0:
+                tr_qk(wi + 1)
+            qk(g + 2)
+            tr_e(g - 1)
+            if j == 3:
+                mx(wi - 1)
+            bias_max(g + 1)
+            if g >= 0 and g % 8 == 1:
+                vprep(g // 8)
+            if j == 2:
+                quant(wi - 1)
+            expo(g)
+            if j == 1:
+                evict_e(2 * (wi - 1) + 1)
+            if j == 3:
+                evict_e(2 * wi)
+            if j == 0:
+                finish(wi - 2)

@@ -25,6 +25,7 @@ NWIN = ROWS * WPR
 NG = NWIN * 4
 NCH = NWIN // 2
 SCALE = 1.0 / math.sqrt(128.0)
+UNSCALE = math.sqrt(128.0)
 FLOPS = 2 * NWIN * 2 * WIN * WIN * C
 
 
@@ -40,14 +41,17 @@ def tile_single_head_split_window_attention_1d_t_kernel(tc, q, k, v, attn_mask, 
         raw = ctx.enter_context(tc.tile_pool(name="raw", bufs=4))
         work = ctx.enter_context(tc.tile_pool(name="work", bufs=3))
         small = ctx.enter_context(tc.tile_pool(name="small", bufs=8))
-        ps_s = ctx.enter_context(tc.psum_pool(name="ps_s", bufs=3))
+        ps_s = ctx.enter_context(tc.psum_pool(name="ps_s", bufs=4))
         ps_e = ctx.enter_context(tc.psum_pool(name="ps_e", bufs=2))
-        ps_o = ctx.enter_context(tc.psum_pool(name="ps_o", bufs=2))
+        ps_o = ctx.enter_context(tc.psum_pool(name="ps_o", bufs=1))
         ps_t = ctx.enter_context(tc.psum_pool(name="ps_t", bufs=1))
 
         ident = const.tile([P, P], BF16, name="ident")
         make_identity(nc, ident[:])
+        ident32 = const.tile([P, P], F32, name="ident32")
+        make_identity(nc, ident32[:])
         bias = const.tile([P, WPR, 4, WIN], BF16, name="bias")
+        biasT = const.tile([P, WPR, 4, WIN], F32, name="biasT")
 
         st = {}
 
@@ -73,9 +77,8 @@ def tile_single_head_split_window_attention_1d_t_kernel(tc, q, k, v, attn_mask, 
             load_rows(k_raw, kv, row, cr)
             if row == 0:
                 load_bias(2 * cr)
-            load_rows(v_raw, vv, row, cr)
-            if row == 0:
                 load_bias(2 * cr + 1)
+            load_rows(v_raw, vv, row, cr)
             st[("q", ch)] = q_raw
             st[("k", ch)] = k_raw
             st[("v", ch)] = v_raw
@@ -115,6 +118,21 @@ def tile_single_head_split_window_attention_1d_t_kernel(tc, q, k, v, attn_mask, 
             nc.scalar.copy(out=qkT[:], in_=tp[:])
             st[("qkT", wi)] = qkT
 
+        def tr_bias(n, half):
+            if n >= WPR:
+                return
+            bp = ps_t.tile([P, 2, 4, P], BF16, tag="tp")
+            for tt in range(2):
+                for j in range(4):
+                    t = 2 * half + tt
+                    nc.tensor.transpose(bp[:, tt, j, :], bias[:, n, j, t * P:(t + 1) * P], ident[:])
+            dst = biasT[:, n, 2 * half:2 * half + 2, :].rearrange("p t x -> p (t x)")
+            src = bp[:].rearrange("p t j x -> p (t j x)")
+            if half == 0:
+                nc.scalar.activation(out=dst, in_=src, func=ACT.Copy, scale=UNSCALE)
+            else:
+                nc.vector.tensor_scalar(out=dst, in0=src, scalar1=UNSCALE, scalar2=None, op0=ALU.mult)
+
         def qk(g):
             if g < 0 or g >= NG:
                 return
@@ -126,8 +144,17 @@ def tile_single_head_split_window_attention_1d_t_kernel(tc, q, k, v, attn_mask, 
                 lhsT=qkT[:, j, :],
                 rhs=qkT[:, 4:8, :].rearrange("c t x -> c (t x)"),
                 start=True,
-                stop=True,
+                stop=False,
             )
+            for t in range(4):
+                nc.tensor.matmul(
+                    s_ps[:, t * P:(t + 1) * P],
+                    lhsT=biasT[:, wi % WPR, t, j * P:(j + 1) * P],
+                    rhs=ident32[:],
+                    start=False,
+                    stop=(t == 3),
+                    is_transpose=True,
+                )
             st[("s_ps", g)] = s_ps
 
         def bias_max(g):
@@ -135,14 +162,10 @@ def tile_single_head_split_window_attention_1d_t_kernel(tc, q, k, v, attn_mask, 
                 return
             wi, j = g // 4, g % 4
             s_ps = st[("s_ps", g)]
-            ns = work.tile([P, WIN], F32, tag="ns", bufs=4)
-            nc.vector.scalar_tensor_tensor(
-                out=ns[:], in0=s_ps[:], scalar=-SCALE, in1=bias[:, wi % WPR, j, :],
-                op0=ALU.mult, op1=ALU.subtract,
-            )
+            mx_t = small.tile([P, 1], F32, tag="mx_t")
+            nc.vector.tensor_reduce(out=mx_t[:], in_=s_ps[:], axis=AX.X, op=ALU.max)
             nm = small.tile([P, 1], F32, tag="nm")
-            nc.vector.tensor_reduce(out=nm[:], in_=ns[:], axis=AX.X, op=ALU.min)
-            st[("ns", g)] = ns
+            nc.gpsimd.tensor_scalar(out=nm[:], in0=mx_t[:], scalar1=-SCALE, scalar2=0.0, op0=ALU.mult, op1=ALU.add)
             st[("nm", g)] = nm
 
         def expo(g):
@@ -153,11 +176,11 @@ def tile_single_head_split_window_attention_1d_t_kernel(tc, q, k, v, attn_mask, 
                 rs_new = small.tile([P, 4], F32, tag="rs")
                 st[("rs", wi)] = rs_new
             rs = st[("rs", wi)]
-            ns = st[("ns", g)]
+            s_ps = st[("s_ps", g)]
             nm = st[("nm", g)]
             e = work.tile([P, WIN], BF16, tag="e", bufs=4)
             nc.scalar.activation(
-                out=e[:], in_=ns[:], func=ACT.Exp, bias=nm[:, 0:1], scale=-1.0,
+                out=e[:], in_=s_ps[:], func=ACT.Exp, bias=nm[:, 0:1], scale=SCALE,
                 accum_out=rs[:, j:j + 1],
             )
             st[("e", g)] = e
@@ -183,10 +206,12 @@ def tile_single_head_split_window_attention_1d_t_kernel(tc, q, k, v, attn_mask, 
                 st[("grp", wi)] = grp_new
             grp = st[("grp", wi)]
             et = st[("et", pr)]
-            nc.scalar.copy(
-                out=grp[:, 256 * hh:256 * (hh + 1), :].rearrange("p (a x) t -> p a x t", a=2),
-                in_=et[:].rearrange("p a t x -> p a x t"),
-            )
+            dst = grp[:, 256 * hh:256 * (hh + 1), :].rearrange("p (a x) t -> p a x t", a=2)
+            src = et[:].rearrange("p a t x -> p a x t")
+            if pr % 4 == 1:
+                nc.vector.tensor_copy(out=dst, in_=src)
+            else:
+                nc.scalar.copy(out=dst, in_=src)
 
         def quant(wi):
             if wi < 0 or wi >= NWIN:
@@ -230,13 +255,9 @@ def tile_single_head_split_window_attention_1d_t_kernel(tc, q, k, v, attn_mask, 
             ri = small.tile([P, 4], F32, tag="ri")
             nc.vector.reciprocal(out=ri[:], in_=rs[:])
             o_sb = work.tile([P, 4, C], F32, tag="o_sb")
-            if wi % 2 == 0:
-                nc.vector.tensor_tensor(
-                    out=o_sb[:], in0=o_ps[:], in1=ri[:].unsqueeze(2).to_broadcast([P, 4, C]), op=ALU.mult,
-                )
-            else:
-                for j in range(4):
-                    nc.scalar.activation(out=o_sb[:, j, :], in_=o_ps[:, j, :], func=ACT.Copy, scale=ri[:, j:j + 1])
+            nc.vector.tensor_tensor(
+                out=o_sb[:], in0=o_ps[:], in1=ri[:].unsqueeze(2).to_broadcast([P, 4, C]), op=ALU.mult,
+            )
             t0 = 2 + 4 * n
             if t0 + 4 <= TPR:
                 nc.sync.dma_start(out=ov[row, :, t0:t0 + 4, :], in_=o_sb[:])
@@ -248,12 +269,20 @@ def tile_single_head_split_window_attention_1d_t_kernel(tc, q, k, v, attn_mask, 
         load_chunk(1)
         load_chunk(2)
         tr_qk(0)
+        tr_bias(0, 0)
+        tr_bias(0, 1)
+        tr_bias(1, 0)
+        tr_bias(1, 1)
         for g in range(-2, NG + 10):
             wi, j = g // 4, g % 4
             if g >= 0 and g % 8 == 0:
                 load_chunk(g // 8 + 3)
             if j == 0 and g >= 0:
                 tr_qk(wi + 1)
+            if j == 1 and g >= 0:
+                tr_bias(wi + 2, 0)
+            if j == 2 and g >= 0:
+                tr_bias(wi + 2, 1)
             qk(g + 2)
             tr_e(g - 1)
             if j == 3:

@@ -25,7 +25,6 @@ NWIN = ROWS * WPR
 NG = NWIN * 4
 NCH = NWIN // 2
 SCALE = 1.0 / math.sqrt(128.0)
-UNSCALE = math.sqrt(128.0)
 FLOPS = 2 * NWIN * 2 * WIN * WIN * C
 
 
@@ -41,17 +40,15 @@ def tile_single_head_split_window_attention_1d_t_kernel(tc, q, k, v, attn_mask, 
         raw = ctx.enter_context(tc.tile_pool(name="raw", bufs=4))
         work = ctx.enter_context(tc.tile_pool(name="work", bufs=3))
         small = ctx.enter_context(tc.tile_pool(name="small", bufs=8))
-        ps_s = ctx.enter_context(tc.psum_pool(name="ps_s", bufs=4))
+        ps_s = ctx.enter_context(tc.psum_pool(name="ps_s", bufs=3))
         ps_e = ctx.enter_context(tc.psum_pool(name="ps_e", bufs=2))
-        ps_o = ctx.enter_context(tc.psum_pool(name="ps_o", bufs=1))
+        ps_o = ctx.enter_context(tc.psum_pool(name="ps_o", bufs=2))
         ps_t = ctx.enter_context(tc.psum_pool(name="ps_t", bufs=1))
+        ctx.enter_context(tc.manual_schedule())
 
         ident = const.tile([P, P], BF16, name="ident")
         make_identity(nc, ident[:])
-        ident32 = const.tile([P, P], F32, name="ident32")
-        make_identity(nc, ident32[:])
         bias = const.tile([P, WPR, 4, WIN], BF16, name="bias")
-        biasT = const.tile([P, WPR, 4, WIN], F32, name="biasT")
 
         st = {}
 
@@ -77,22 +74,28 @@ def tile_single_head_split_window_attention_1d_t_kernel(tc, q, k, v, attn_mask, 
             load_rows(k_raw, kv, row, cr)
             if row == 0:
                 load_bias(2 * cr)
-                load_bias(2 * cr + 1)
             load_rows(v_raw, vv, row, cr)
+            if row == 0:
+                load_bias(2 * cr + 1)
             st[("q", ch)] = q_raw
             st[("k", ch)] = k_raw
             st[("v", ch)] = v_raw
 
-        def vprep(ch):
+        def vregroup(ch):
             if ch >= NCH:
                 return
             v_raw = st[("v", ch)]
-            vg = work.tile([P, 2, C, 4], BF16, tag="vg", align_bytes=64)
-            for a in range(2):
-                nc.vector.tensor_copy(
-                    out=vg[:, a, :, :],
-                    in_=v_raw[:, 4 * a:4 * a + 4, :].rearrange("p t c -> p c t"),
-                )
+            vg = work.tile([P, 2, C, 4], BF16, tag="vg", bufs=2, align_bytes=64)
+            nc.gpsimd.tensor_scalar(
+                out=vg[:], in0=v_raw[:].rearrange("p (a t) c -> p a c t", a=2),
+                scalar1=1.0, scalar2=0.0, op0=ALU.mult, op1=ALU.add,
+            )
+            st[("vg", ch)] = vg
+
+        def vquant(ch):
+            if ch >= NCH:
+                return
+            vg = st[("vg", ch)]
             vc = work.tile([P, 2 * C], U32, tag="vc", align_bytes=64)
             vs = work.tile([P, 2 * C], U8, tag="vs", align_bytes=64)
             nc.vector.quantize_mx(
@@ -118,21 +121,6 @@ def tile_single_head_split_window_attention_1d_t_kernel(tc, q, k, v, attn_mask, 
             nc.scalar.copy(out=qkT[:], in_=tp[:])
             st[("qkT", wi)] = qkT
 
-        def tr_bias(n, half):
-            if n >= WPR:
-                return
-            bp = ps_t.tile([P, 2, 4, P], BF16, tag="tp")
-            for tt in range(2):
-                for j in range(4):
-                    t = 2 * half + tt
-                    nc.tensor.transpose(bp[:, tt, j, :], bias[:, n, j, t * P:(t + 1) * P], ident[:])
-            dst = biasT[:, n, 2 * half:2 * half + 2, :].rearrange("p t x -> p (t x)")
-            src = bp[:].rearrange("p t j x -> p (t j x)")
-            if half == 0:
-                nc.scalar.activation(out=dst, in_=src, func=ACT.Copy, scale=UNSCALE)
-            else:
-                nc.vector.tensor_scalar(out=dst, in0=src, scalar1=UNSCALE, scalar2=None, op0=ALU.mult)
-
         def qk(g):
             if g < 0 or g >= NG:
                 return
@@ -144,28 +132,28 @@ def tile_single_head_split_window_attention_1d_t_kernel(tc, q, k, v, attn_mask, 
                 lhsT=qkT[:, j, :],
                 rhs=qkT[:, 4:8, :].rearrange("c t x -> c (t x)"),
                 start=True,
-                stop=False,
+                stop=True,
             )
-            for t in range(4):
-                nc.tensor.matmul(
-                    s_ps[:, t * P:(t + 1) * P],
-                    lhsT=biasT[:, wi % WPR, t, j * P:(j + 1) * P],
-                    rhs=ident32[:],
-                    start=False,
-                    stop=(t == 3),
-                    is_transpose=True,
-                )
             st[("s_ps", g)] = s_ps
 
-        def bias_max(g):
+        def add_bias(g):
             if g < 0 or g >= NG:
                 return
             wi, j = g // 4, g % 4
             s_ps = st[("s_ps", g)]
-            mx_t = small.tile([P, 1], F32, tag="mx_t")
-            nc.vector.tensor_reduce(out=mx_t[:], in_=s_ps[:], axis=AX.X, op=ALU.max)
+            ns = work.tile([P, WIN], F32, tag="ns", bufs=4)
+            nc.vector.scalar_tensor_tensor(
+                out=ns[:], in0=s_ps[:], scalar=-SCALE, in1=bias[:, wi % WPR, j, :],
+                op0=ALU.mult, op1=ALU.subtract,
+            )
+            st[("ns", g)] = ns
+
+        def row_max(g):
+            if g < 0 or g >= NG:
+                return
+            ns = st[("ns", g)]
             nm = small.tile([P, 1], F32, tag="nm")
-            nc.gpsimd.tensor_scalar(out=nm[:], in0=mx_t[:], scalar1=-SCALE, scalar2=0.0, op0=ALU.mult, op1=ALU.add)
+            nc.vector.tensor_reduce(out=nm[:], in_=ns[:], axis=AX.X, op=ALU.min)
             st[("nm", g)] = nm
 
         def expo(g):
@@ -176,11 +164,11 @@ def tile_single_head_split_window_attention_1d_t_kernel(tc, q, k, v, attn_mask, 
                 rs_new = small.tile([P, 4], F32, tag="rs")
                 st[("rs", wi)] = rs_new
             rs = st[("rs", wi)]
-            s_ps = st[("s_ps", g)]
+            ns = st[("ns", g)]
             nm = st[("nm", g)]
             e = work.tile([P, WIN], BF16, tag="e", bufs=4)
             nc.scalar.activation(
-                out=e[:], in_=s_ps[:], func=ACT.Exp, bias=nm[:, 0:1], scale=SCALE,
+                out=e[:], in_=ns[:], func=ACT.Exp, bias=nm[:, 0:1], scale=-1.0,
                 accum_out=rs[:, j:j + 1],
             )
             st[("e", g)] = e
@@ -200,18 +188,25 @@ def tile_single_head_split_window_attention_1d_t_kernel(tc, q, k, v, attn_mask, 
         def evict_e(pr):
             if pr < 0 or pr >= NG // 2:
                 return
+            et = st[("et", pr)]
+            ets = work.tile([P, 2, 4, P], BF16, tag="ets")
+            nc.scalar.copy(out=ets[:], in_=et[:])
+            st[("ets", pr)] = ets
+
+        def regroup(pr):
+            if pr < 0 or pr >= NG // 2:
+                return
             wi, hh = pr // 2, pr % 2
             if hh == 0:
-                grp_new = work.tile([P, WIN, 4], BF16, tag="grp", align_bytes=64)
+                grp_new = work.tile([P, WIN, 4], BF16, tag="grp", bufs=1, align_bytes=64)
                 st[("grp", wi)] = grp_new
             grp = st[("grp", wi)]
-            et = st[("et", pr)]
-            dst = grp[:, 256 * hh:256 * (hh + 1), :].rearrange("p (a x) t -> p a x t", a=2)
-            src = et[:].rearrange("p a t x -> p a x t")
-            if pr % 4 == 1:
-                nc.vector.tensor_copy(out=dst, in_=src)
-            else:
-                nc.scalar.copy(out=dst, in_=src)
+            ets = st[("ets", pr)]
+            nc.gpsimd.tensor_scalar(
+                out=grp[:, 256 * hh:256 * (hh + 1), :].rearrange("p (a x) t -> p a x t", a=2),
+                in0=ets[:].rearrange("p a t x -> p a x t"),
+                scalar1=1.0, scalar2=0.0, op0=ALU.mult, op1=ALU.add,
+            )
 
         def quant(wi):
             if wi < 0 or wi >= NWIN:
@@ -246,18 +241,23 @@ def tile_single_head_split_window_attention_1d_t_kernel(tc, q, k, v, attn_mask, 
                 )
             st[("o_ps", wi)] = o_ps
 
+        def recip(wi):
+            if wi < 0 or wi >= NWIN:
+                return
+            rs = st[("rs", wi)]
+            ri = small.tile([P, 4], F32, tag="ri")
+            nc.vector.reciprocal(out=ri[:], in_=rs[:])
+            st[("ri", wi)] = ri
+
         def finish(wi):
             if wi < 0 or wi >= NWIN:
                 return
             row, n = wi // WPR, wi % WPR
             o_ps = st[("o_ps", wi)]
-            rs = st[("rs", wi)]
-            ri = small.tile([P, 4], F32, tag="ri")
-            nc.vector.reciprocal(out=ri[:], in_=rs[:])
+            ri = st[("ri", wi)]
             o_sb = work.tile([P, 4, C], F32, tag="o_sb")
-            nc.vector.tensor_tensor(
-                out=o_sb[:], in0=o_ps[:], in1=ri[:].unsqueeze(2).to_broadcast([P, 4, C]), op=ALU.mult,
-            )
+            for j in range(4):
+                nc.scalar.activation(out=o_sb[:, j, :], in_=o_ps[:, j, :], func=ACT.Copy, scale=ri[:, j:j + 1])
             t0 = 2 + 4 * n
             if t0 + 4 <= TPR:
                 nc.sync.dma_start(out=ov[row, :, t0:t0 + 4, :], in_=o_sb[:])
@@ -265,37 +265,40 @@ def tile_single_head_split_window_attention_1d_t_kernel(tc, q, k, v, attn_mask, 
                 nc.sync.dma_start(out=ov[row, :, t0:TPR, :], in_=o_sb[:, 0:2, :])
                 nc.sync.dma_start(out=ov[row, :, 0:2, :], in_=o_sb[:, 2:4, :])
 
+        L_TQ, L_Q, L_A, L_R, L_TE, L_EV, L_QN, L_MX, L_FIN = 5, 3, 2, 1, 1, 1, 2, 1, 1
         load_chunk(0)
         load_chunk(1)
         load_chunk(2)
+        vregroup(0)
         tr_qk(0)
-        tr_bias(0, 0)
-        tr_bias(0, 1)
-        tr_bias(1, 0)
-        tr_bias(1, 1)
-        for g in range(-2, NG + 10):
-            wi, j = g // 4, g % 4
+        for g in range(-5, NG + 24):
             if g >= 0 and g % 8 == 0:
                 load_chunk(g // 8 + 3)
-            if j == 0 and g >= 0:
-                tr_qk(wi + 1)
-            if j == 1 and g >= 0:
-                tr_bias(wi + 2, 0)
-            if j == 2 and g >= 0:
-                tr_bias(wi + 2, 1)
-            qk(g + 2)
-            tr_e(g - 1)
-            if j == 3:
-                mx(wi - 1)
-            bias_max(g + 1)
-            if g >= 0 and g % 8 == 1:
-                vprep(g // 8)
-            if j == 2:
-                quant(wi - 1)
+            x = g + L_TQ
+            if x >= 4 and x % 4 == 0:
+                tr_qk(x // 4)
+            qk(g + L_Q)
+            tr_e(g - L_TE)
+            x = g - L_TE - L_EV - L_QN - L_MX
+            if x >= 0 and x % 4 == 3:
+                mx(x // 4)
+            add_bias(g + L_A)
+            row_max(g + L_R)
+            x = g - L_TE - L_EV - L_QN
+            if x >= 0 and x % 4 == 3:
+                if (x // 4) % 2 == 0:
+                    vquant(x // 8)
+                quant(x // 4)
+                recip(x // 4)
+            x = g - L_TE - L_EV
+            if x >= 0 and x % 2 == 1:
+                evict_e(x // 2)
             expo(g)
-            if j == 1:
-                evict_e(2 * (wi - 1) + 1)
-            if j == 3:
-                evict_e(2 * wi)
-            if j == 0:
-                finish(wi - 2)
+            x = g - L_TE - L_EV - L_QN - L_MX - L_FIN
+            if x >= 0 and x % 4 == 3:
+                finish(x // 4)
+            x = g - L_TE - L_EV
+            if x >= 0 and x % 2 == 1:
+                regroup(x // 2)
+            if x >= 0 and x % 8 == 1:
+                vregroup(x // 8 + 1)

@@ -25,6 +25,7 @@ NWIN = ROWS * WPR
 NG = NWIN * 4
 NCH = NWIN // 2
 SCALE = 1.0 / math.sqrt(128.0)
+UNSCALE = math.sqrt(128.0)
 FLOPS = 2 * NWIN * 2 * WIN * WIN * C
 
 
@@ -42,26 +43,36 @@ def tile_single_head_split_window_attention_1d_t_kernel(tc, q, k, v, attn_mask, 
         small = ctx.enter_context(tc.tile_pool(name="small", bufs=8))
         ps_s = ctx.enter_context(tc.psum_pool(name="ps_s", bufs=3))
         ps_e = ctx.enter_context(tc.psum_pool(name="ps_e", bufs=2))
-        ps_o = ctx.enter_context(tc.psum_pool(name="ps_o", bufs=2))
+        ps_x = ctx.enter_context(tc.psum_pool(name="ps_x", bufs=1))
+        ps_o = ctx.enter_context(tc.psum_pool(name="ps_o", bufs=1))
         ps_t = ctx.enter_context(tc.psum_pool(name="ps_t", bufs=1))
         ctx.enter_context(tc.manual_schedule())
 
         ident = const.tile([P, P], BF16, name="ident")
         make_identity(nc, ident[:])
+        ident32 = const.tile([P, P], F32, name="ident32")
+        make_identity(nc, ident32[:])
         bias = const.tile([P, WPR, 4, WIN], BF16, name="bias")
+        biasT = const.tile([P, WPR, 4, P], F32, name="biasT")
+
+        def in_psum(g):
+            return g >= 4 * WPR and g % 4 == 0
 
         st = {}
 
-        def load_rows(dst, src, row, ch_in_row):
+        def load_rows(dst, src, row, ch_in_row, lo, hi):
             t0 = 2 + 8 * ch_in_row
-            if t0 + 8 <= TPR:
-                nc.sync.dma_start(out=dst[:, :, :], in_=src[row, :, t0:t0 + 8, :])
+            if t0 + hi <= TPR:
+                nc.sync.dma_start(out=dst[:, lo:hi, :], in_=src[row, :, t0 + lo:t0 + hi, :])
             else:
                 nc.sync.dma_start(out=dst[:, 0:6, :], in_=src[row, :, t0:TPR, :])
                 nc.sync.dma_start(out=dst[:, 6:8, :], in_=src[row, :, 0:2, :])
 
-        def load_bias(n):
-            nc.sync.dma_start(out=bias[:, n, :, :], in_=attn_mask[n].rearrange("(j p) x -> p j x", p=P))
+        def load_bias(n, lo, hi):
+            nc.sync.dma_start(
+                out=bias[:, n, lo:hi, :],
+                in_=attn_mask[n, lo * P:hi * P, :].rearrange("(j p) x -> p j x", p=P),
+            )
 
         def load_chunk(ch):
             if ch >= NCH:
@@ -70,13 +81,22 @@ def tile_single_head_split_window_attention_1d_t_kernel(tc, q, k, v, attn_mask, 
             q_raw = raw.tile([P, 8, C], BF16, tag="q_raw")
             k_raw = raw.tile([P, 8, C], BF16, tag="k_raw")
             v_raw = raw.tile([P, 8, C], BF16, tag="v_raw")
-            load_rows(q_raw, qv, row, cr)
-            load_rows(k_raw, kv, row, cr)
-            if row == 0:
-                load_bias(2 * cr)
-            load_rows(v_raw, vv, row, cr)
-            if row == 0:
-                load_bias(2 * cr + 1)
+            if ch == 0:
+                load_rows(q_raw, qv, row, cr, 0, 4)
+                load_rows(k_raw, kv, row, cr, 0, 4)
+                load_bias(0, 0, 1)
+                load_bias(0, 1, 4)
+                load_rows(q_raw, qv, row, cr, 4, 8)
+                load_rows(k_raw, kv, row, cr, 4, 8)
+                load_bias(1, 0, 4)
+                load_rows(v_raw, vv, row, cr, 0, 8)
+            else:
+                load_rows(q_raw, qv, row, cr, 0, 8)
+                load_rows(k_raw, kv, row, cr, 0, 8)
+                if row == 0:
+                    load_bias(2 * cr, 0, 4)
+                    load_bias(2 * cr + 1, 0, 4)
+                load_rows(v_raw, vv, row, cr, 0, 8)
             st[("q", ch)] = q_raw
             st[("k", ch)] = k_raw
             st[("v", ch)] = v_raw
@@ -106,7 +126,7 @@ def tile_single_head_split_window_attention_1d_t_kernel(tc, q, k, v, attn_mask, 
             st[("vc", ch)] = vc
             st[("vs", ch)] = vs
 
-        def tr_qk(wi):
+        def tqk_pe(wi):
             if wi >= NWIN:
                 return
             ch, a = wi // 2, wi % 2
@@ -117,28 +137,58 @@ def tile_single_head_split_window_attention_1d_t_kernel(tc, q, k, v, attn_mask, 
                 nc.tensor.transpose(tp[:, j, :], q_raw[:, 4 * a + j, :], ident[:])
             for j in range(4):
                 nc.tensor.transpose(tp[:, 4 + j, :], k_raw[:, 4 * a + j, :], ident[:])
-            qkT = work.tile([P, 8, P], BF16, tag="qkT")
+            st[("tp", wi)] = tp
+
+        def tqk_ev(wi):
+            if wi >= NWIN:
+                return
+            tp = st[("tp", wi)]
+            qkT = work.tile([P, 8, P], BF16, tag="qkT", bufs=4)
             nc.scalar.copy(out=qkT[:], in_=tp[:])
             st[("qkT", wi)] = qkT
 
+        def tb_pe(r):
+            bp = ps_t.tile([P, 2, 4, P], BF16, tag="tp")
+            for a in range(2):
+                for t in range(4):
+                    nc.tensor.transpose(bp[:, a, t, :], bias[:, 2 * r + a, 0, t * P:(t + 1) * P], ident[:])
+            st[("bp", r)] = bp
+
+        def tb_ev(r):
+            bp = st[("bp", r)]
+            nc.scalar.activation(
+                out=biasT[:, 2 * r:2 * r + 2, :, :].rearrange("p a t x -> p (a t x)"),
+                in_=bp[:].rearrange("p a t x -> p (a t x)"),
+                func=ACT.Copy, scale=UNSCALE,
+            )
+
         def qk(g):
-            if g < 0 or g >= NG:
-                return
             wi, j = g // 4, g % 4
             qkT = st[("qkT", wi)]
-            s_ps = ps_s.tile([P, WIN], F32, tag="s_ps")
+            if in_psum(g):
+                s_ps = ps_x.tile([P, WIN], F32, tag="sx")
+            else:
+                s_ps = ps_s.tile([P, WIN], F32, tag="s_ps")
             nc.tensor.matmul(
                 s_ps[:],
                 lhsT=qkT[:, j, :],
                 rhs=qkT[:, 4:8, :].rearrange("c t x -> c (t x)"),
                 start=True,
-                stop=True,
+                stop=not in_psum(g),
             )
+            if in_psum(g):
+                for t in range(4):
+                    nc.tensor.matmul(
+                        s_ps[:, t * P:(t + 1) * P],
+                        lhsT=biasT[:, wi % WPR, t, :],
+                        rhs=ident32[:],
+                        start=False,
+                        stop=(t == 3),
+                        is_transpose=True,
+                    )
             st[("s_ps", g)] = s_ps
 
         def add_bias(g):
-            if g < 0 or g >= NG:
-                return
             wi, j = g // 4, g % 4
             s_ps = st[("s_ps", g)]
             ns = work.tile([P, WIN], F32, tag="ns", bufs=4)
@@ -149,12 +199,19 @@ def tile_single_head_split_window_attention_1d_t_kernel(tc, q, k, v, attn_mask, 
             st[("ns", g)] = ns
 
         def row_max(g):
-            if g < 0 or g >= NG:
-                return
-            ns = st[("ns", g)]
-            nm = small.tile([P, 1], F32, tag="nm")
-            nc.vector.tensor_reduce(out=nm[:], in_=ns[:], axis=AX.X, op=ALU.min)
-            st[("nm", g)] = nm
+            if in_psum(g):
+                mx_t = small.tile([P, 1], F32, tag="mx_t")
+                nc.vector.tensor_reduce(out=mx_t[:], in_=st[("s_ps", g)][:], axis=AX.X, op=ALU.max)
+                st[("mx_t", g)] = mx_t
+            else:
+                nm = small.tile([P, 1], F32, tag="nm")
+                nc.vector.tensor_reduce(out=nm[:], in_=st[("ns", g)][:], axis=AX.X, op=ALU.min)
+                st[("nm", g)] = nm
+
+        def scale_max(g):
+            nmx = small.tile([P, 1], F32, tag="nmx")
+            nc.scalar.mul(out=nmx[:], in_=st[("mx_t", g)][:], mul=-SCALE)
+            st[("nm", g)] = nmx
 
         def expo(g):
             if g < 0 or g >= NG:
@@ -164,13 +221,18 @@ def tile_single_head_split_window_attention_1d_t_kernel(tc, q, k, v, attn_mask, 
                 rs_new = small.tile([P, 4], F32, tag="rs")
                 st[("rs", wi)] = rs_new
             rs = st[("rs", wi)]
-            ns = st[("ns", g)]
             nm = st[("nm", g)]
             e = work.tile([P, WIN], BF16, tag="e", bufs=4)
-            nc.scalar.activation(
-                out=e[:], in_=ns[:], func=ACT.Exp, bias=nm[:, 0:1], scale=-1.0,
-                accum_out=rs[:, j:j + 1],
-            )
+            if in_psum(g):
+                nc.scalar.activation(
+                    out=e[:], in_=st[("s_ps", g)][:], func=ACT.Exp, bias=nm[:, 0:1], scale=SCALE,
+                    accum_out=rs[:, j:j + 1],
+                )
+            else:
+                nc.scalar.activation(
+                    out=e[:], in_=st[("ns", g)][:], func=ACT.Exp, bias=nm[:, 0:1], scale=-1.0,
+                    accum_out=rs[:, j:j + 1],
+                )
             st[("e", g)] = e
 
         def tr_e(g):
@@ -196,44 +258,44 @@ def tile_single_head_split_window_attention_1d_t_kernel(tc, q, k, v, attn_mask, 
         def regroup(pr):
             if pr < 0 or pr >= NG // 2:
                 return
-            wi, hh = pr // 2, pr % 2
-            if hh == 0:
-                grp_new = work.tile([P, WIN, 4], BF16, tag="grp", bufs=1, align_bytes=64)
-                st[("grp", wi)] = grp_new
-            grp = st[("grp", wi)]
+            ch, pos = pr // 4, pr % 4
+            if pos == 0:
+                grp_new = work.tile([P, 2 * WIN, 4], BF16, tag="grp", bufs=1, align_bytes=64)
+                st[("grp", ch)] = grp_new
+            grp = st[("grp", ch)]
             ets = st[("ets", pr)]
             nc.gpsimd.tensor_scalar(
-                out=grp[:, 256 * hh:256 * (hh + 1), :].rearrange("p (a x) t -> p a x t", a=2),
+                out=grp[:, 256 * pos:256 * (pos + 1), :].rearrange("p (a x) t -> p a x t", a=2),
                 in0=ets[:].rearrange("p a t x -> p a x t"),
                 scalar1=1.0, scalar2=0.0, op0=ALU.mult, op1=ALU.add,
             )
 
-        def quant(wi):
-            if wi < 0 or wi >= NWIN:
+        def quant(ch):
+            if ch < 0 or ch >= NCH:
                 return
-            grp = st[("grp", wi)]
-            ec = work.tile([P, WIN], U32, tag="ec", align_bytes=64)
-            es = work.tile([P, WIN], U8, tag="es", align_bytes=64)
+            grp = st[("grp", ch)]
+            ec = work.tile([P, 2 * WIN], U32, tag="ec", bufs=2, align_bytes=64)
+            es = work.tile([P, 2 * WIN], U8, tag="es", bufs=2, align_bytes=64)
             nc.vector.quantize_mx(
                 out=ec[:].bitcast(FP8X4), scales=es[:], in_=grp[:].rearrange("p x t -> p (x t)"),
             )
-            st[("ec", wi)] = ec
-            st[("es", wi)] = es
+            st[("ec", ch)] = ec
+            st[("es", ch)] = es
 
         def mx(wi):
             if wi < 0 or wi >= NWIN:
                 return
             ch, a = wi // 2, wi % 2
-            ec = st[("ec", wi)]
-            es = st[("es", wi)]
+            ec = st[("ec", ch)]
+            es = st[("es", ch)]
             vc = st[("vc", ch)]
             vs = st[("vs", ch)]
             o_ps = ps_o.tile([P, 4, C], F32, tag="o_ps")
             for j in range(4):
                 nc.tensor.matmul_mx(
                     out=o_ps[:, j, :],
-                    lhsT=ec[:, j * P:(j + 1) * P].bitcast(FP8X4),
-                    lhsT_scale=es[:, j * P:(j + 1) * P],
+                    lhsT=ec[:, (4 * a + j) * P:(4 * a + j + 1) * P].bitcast(FP8X4),
+                    lhsT_scale=es[:, (4 * a + j) * P:(4 * a + j + 1) * P],
                     rhs=vc[:, a * C:(a + 1) * C].bitcast(FP8X4),
                     rhs_scale=vs[:, a * C:(a + 1) * C],
                     start=True,
@@ -265,40 +327,70 @@ def tile_single_head_split_window_attention_1d_t_kernel(tc, q, k, v, attn_mask, 
                 nc.sync.dma_start(out=ov[row, :, t0:TPR, :], in_=o_sb[:, 0:2, :])
                 nc.sync.dma_start(out=ov[row, :, 0:2, :], in_=o_sb[:, 2:4, :])
 
-        L_TQ, L_Q, L_A, L_R, L_TE, L_EV, L_QN, L_MX, L_FIN = 5, 3, 2, 1, 1, 1, 2, 1, 1
         load_chunk(0)
         load_chunk(1)
         load_chunk(2)
         vregroup(0)
-        tr_qk(0)
-        for g in range(-5, NG + 24):
+        vregroup(1)
+        tqk_pe(0)
+        tqk_ev(0)
+        tqk_pe(1)
+        tqk_ev(1)
+        for g in range(-4, NG + 24):
             if g >= 0 and g % 8 == 0:
                 load_chunk(g // 8 + 3)
-            x = g + L_TQ
-            if x >= 4 and x % 4 == 0:
-                tr_qk(x // 4)
-            qk(g + L_Q)
-            tr_e(g - L_TE)
-            x = g - L_TE - L_EV - L_QN - L_MX
-            if x >= 0 and x % 4 == 3:
-                mx(x // 4)
-            add_bias(g + L_A)
-            row_max(g + L_R)
-            x = g - L_TE - L_EV - L_QN
-            if x >= 0 and x % 4 == 3:
-                if (x // 4) % 2 == 0:
-                    vquant(x // 8)
-                quant(x // 4)
-                recip(x // 4)
-            x = g - L_TE - L_EV
-            if x >= 0 and x % 2 == 1:
+            x = g + 9
+            if x >= 8 and x % 4 == 0:
+                tqk_pe(x // 4)
+            if 0 <= g < 32 and g % 8 == 1:
+                tb_pe(g // 8)
+            x = g + 3
+            if 0 <= x < NG and not in_psum(x):
+                qk(x)
+            x = g + 2
+            if 0 <= x < NG and in_psum(x):
+                qk(x)
+            tr_e(g - 1)
+            x = g - 12
+            if x >= 0 and x % 8 == 0:
+                mx(2 * (x // 8))
+            x = g - 16
+            if x >= 0 and x % 8 == 0:
+                mx(2 * (x // 8) + 1)
+            x = g + 2
+            if 0 <= x < NG and not in_psum(x):
+                add_bias(x)
+            x = g + 1
+            if 0 <= x < NG:
+                row_max(x)
+            x = g - 9
+            if x >= 0 and x % 8 == 0:
+                vquant(x // 8)
+            x = g - 11
+            if x >= 0 and x % 8 == 0:
+                quant(x // 8)
+                recip(2 * (x // 8))
+                recip(2 * (x // 8) + 1)
+            if 0 <= g < NG and in_psum(g):
+                scale_max(g)
+            x = g + 8
+            if x >= 8 and x % 4 == 0:
+                tqk_ev(x // 4)
+            if 0 <= g < 32 and g % 8 == 2:
+                tb_ev(g // 8)
+            x = g - 3
+            if x >= 0 and x % 2 == 0:
                 evict_e(x // 2)
+            x = g - 14
+            if x >= 0 and x % 8 == 0:
+                finish(2 * (x // 8))
+            x = g - 18
+            if x >= 0 and x % 8 == 0:
+                finish(2 * (x // 8) + 1)
             expo(g)
-            x = g - L_TE - L_EV - L_QN - L_MX - L_FIN
-            if x >= 0 and x % 4 == 3:
-                finish(x // 4)
-            x = g - L_TE - L_EV
-            if x >= 0 and x % 2 == 1:
+            x = g - 3
+            if x >= 0 and x % 2 == 0:
                 regroup(x // 2)
-            if x >= 0 and x % 8 == 1:
-                vregroup(x // 8 + 1)
+            x = g - 11
+            if x >= 0 and x % 8 == 0:
+                vregroup(x // 8 + 2)

@@ -62,11 +62,11 @@ def tile_single_head_split_window_attention_1d_t_kernel(tc, q, k, v, attn_mask, 
 
         def load_rows(dst, src, row, ch_in_row, lo, hi):
             t0 = 2 + 8 * ch_in_row
-            if t0 + hi <= TPR:
-                nc.sync.dma_start(out=dst[:, lo:hi, :], in_=src[row, :, t0 + lo:t0 + hi, :])
-            else:
-                nc.sync.dma_start(out=dst[:, 0:6, :], in_=src[row, :, t0:TPR, :])
-                nc.sync.dma_start(out=dst[:, 6:8, :], in_=src[row, :, 0:2, :])
+            cut = min(max(TPR - t0, lo), hi)
+            if cut > lo:
+                nc.sync.dma_start(out=dst[:, lo:cut, :], in_=src[row, :, t0 + lo:t0 + cut, :])
+            if hi > cut:
+                nc.sync.dma_start(out=dst[:, cut:hi, :], in_=src[row, :, t0 + cut - TPR:t0 + hi - TPR, :])
 
         def load_bias(n, lo, hi):
             nc.sync.dma_start(
@@ -81,22 +81,19 @@ def tile_single_head_split_window_attention_1d_t_kernel(tc, q, k, v, attn_mask, 
             q_raw = raw.tile([P, 8, C], BF16, tag="q_raw")
             k_raw = raw.tile([P, 8, C], BF16, tag="k_raw")
             v_raw = raw.tile([P, 8, C], BF16, tag="v_raw")
-            if ch == 0:
-                load_rows(q_raw, qv, row, cr, 0, 4)
-                load_rows(k_raw, kv, row, cr, 0, 4)
-                load_bias(0, 0, 1)
-                load_bias(0, 1, 4)
-                load_rows(q_raw, qv, row, cr, 4, 8)
-                load_rows(k_raw, kv, row, cr, 4, 8)
-                load_bias(1, 0, 4)
-                load_rows(v_raw, vv, row, cr, 0, 8)
+            if row == 0:
+                for a in range(2):
+                    load_rows(q_raw, qv, row, cr, 4 * a, 4 * a + 4)
+                    load_rows(k_raw, kv, row, cr, 4 * a, 4 * a + 4)
+                    if ch == 0 and a == 0:
+                        load_bias(0, 0, 1)
+                        load_bias(0, 1, 4)
+                    else:
+                        load_bias(2 * cr + a, 0, 4)
             else:
                 load_rows(q_raw, qv, row, cr, 0, 8)
                 load_rows(k_raw, kv, row, cr, 0, 8)
-                if row == 0:
-                    load_bias(2 * cr, 0, 4)
-                    load_bias(2 * cr + 1, 0, 4)
-                load_rows(v_raw, vv, row, cr, 0, 8)
+            load_rows(v_raw, vv, row, cr, 0, 8)
             st[("q", ch)] = q_raw
             st[("k", ch)] = k_raw
             st[("v", ch)] = v_raw
@@ -270,6 +267,29 @@ def tile_single_head_split_window_attention_1d_t_kernel(tc, q, k, v, attn_mask, 
                 scalar1=1.0, scalar2=0.0, op0=ALU.mult, op1=ALU.add,
             )
 
+        def evict_direct(pr):
+            ch, pos = pr // 4, pr % 4
+            grp = st[("grp", ch)]
+            et = st[("et", pr)]
+            nc.vector.tensor_copy(
+                out=grp[:, 256 * pos:256 * (pos + 1), :].rearrange("p (a x) t -> p a x t", a=2),
+                in_=et[:].rearrange("p a t x -> p a x t"),
+            )
+
+        def quant_window(wi):
+            ch, a = wi // 2, wi % 2
+            grp = st[("grp", ch)]
+            if a == 0:
+                ec_new = work.tile([P, 2 * WIN], U32, tag="ec", bufs=2, align_bytes=64)
+                es_new = work.tile([P, 2 * WIN], U8, tag="es", bufs=2, align_bytes=64)
+                st[("ec", ch)] = ec_new
+                st[("es", ch)] = es_new
+            nc.vector.quantize_mx(
+                out=st[("ec", ch)][:, a * WIN:(a + 1) * WIN].bitcast(FP8X4),
+                scales=st[("es", ch)][:, a * WIN:(a + 1) * WIN],
+                in_=grp[:, a * WIN:(a + 1) * WIN, :].rearrange("p x t -> p (x t)"),
+            )
+
         def quant(ch):
             if ch < 0 or ch >= NCH:
                 return
@@ -282,15 +302,16 @@ def tile_single_head_split_window_attention_1d_t_kernel(tc, q, k, v, attn_mask, 
             st[("ec", ch)] = ec
             st[("es", ch)] = es
 
-        def mx(wi):
-            if wi < 0 or wi >= NWIN:
-                return
+        def mx(wi, spare_bank=False):
             ch, a = wi // 2, wi % 2
             ec = st[("ec", ch)]
             es = st[("es", ch)]
             vc = st[("vc", ch)]
             vs = st[("vs", ch)]
-            o_ps = ps_o.tile([P, 4, C], F32, tag="o_ps")
+            if spare_bank:
+                o_ps = ps_x.tile([P, 4, C], F32, tag="sx")
+            else:
+                o_ps = ps_o.tile([P, 4, C], F32, tag="o_ps")
             for j in range(4):
                 nc.tensor.matmul_mx(
                     out=o_ps[:, j, :],
@@ -311,15 +332,18 @@ def tile_single_head_split_window_attention_1d_t_kernel(tc, q, k, v, attn_mask, 
             nc.vector.reciprocal(out=ri[:], in_=rs[:])
             st[("ri", wi)] = ri
 
-        def finish(wi):
-            if wi < 0 or wi >= NWIN:
-                return
+        def finish(wi, on_vector=False):
             row, n = wi // WPR, wi % WPR
             o_ps = st[("o_ps", wi)]
             ri = st[("ri", wi)]
             o_sb = work.tile([P, 4, C], F32, tag="o_sb")
-            for j in range(4):
-                nc.scalar.activation(out=o_sb[:, j, :], in_=o_ps[:, j, :], func=ACT.Copy, scale=ri[:, j:j + 1])
+            if on_vector:
+                nc.vector.tensor_tensor(
+                    out=o_sb[:], in0=o_ps[:], in1=ri[:].unsqueeze(2).to_broadcast([P, 4, C]), op=ALU.mult,
+                )
+            else:
+                for j in range(4):
+                    nc.scalar.activation(out=o_sb[:, j, :], in_=o_ps[:, j, :], func=ACT.Copy, scale=ri[:, j:j + 1])
             t0 = 2 + 4 * n
             if t0 + 4 <= TPR:
                 nc.sync.dma_start(out=ov[row, :, t0:t0 + 4, :], in_=o_sb[:])
@@ -327,20 +351,17 @@ def tile_single_head_split_window_attention_1d_t_kernel(tc, q, k, v, attn_mask, 
                 nc.sync.dma_start(out=ov[row, :, t0:TPR, :], in_=o_sb[:, 0:2, :])
                 nc.sync.dma_start(out=ov[row, :, 0:2, :], in_=o_sb[:, 2:4, :])
 
+        LAST = NCH - 1
         load_chunk(0)
         load_chunk(1)
         load_chunk(2)
-        vregroup(0)
-        vregroup(1)
         tqk_pe(0)
         tqk_ev(0)
-        tqk_pe(1)
-        tqk_ev(1)
-        for g in range(-4, NG + 24):
+        for g in range(-4, NG + 20):
             if g >= 0 and g % 8 == 0:
                 load_chunk(g // 8 + 3)
-            x = g + 9
-            if x >= 8 and x % 4 == 0:
+            x = g + 5
+            if x >= 4 and x % 4 == 0:
                 tqk_pe(x // 4)
             if 0 <= g < 32 and g % 8 == 1:
                 tb_pe(g // 8)
@@ -352,10 +373,10 @@ def tile_single_head_split_window_attention_1d_t_kernel(tc, q, k, v, attn_mask, 
                 qk(x)
             tr_e(g - 1)
             x = g - 12
-            if x >= 0 and x % 8 == 0:
+            if x >= 0 and x % 8 == 0 and x // 8 < LAST:
                 mx(2 * (x // 8))
             x = g - 16
-            if x >= 0 and x % 8 == 0:
+            if x >= 0 and x % 8 == 0 and x // 8 < LAST:
                 mx(2 * (x // 8) + 1)
             x = g + 2
             if 0 <= x < NG and not in_psum(x):
@@ -363,34 +384,51 @@ def tile_single_head_split_window_attention_1d_t_kernel(tc, q, k, v, attn_mask, 
             x = g + 1
             if 0 <= x < NG:
                 row_max(x)
-            x = g - 9
-            if x >= 0 and x % 8 == 0:
-                vquant(x // 8)
             x = g - 11
-            if x >= 0 and x % 8 == 0:
+            if x >= 0 and x % 8 == 0 and x // 8 < LAST:
+                vquant(x // 8)
                 quant(x // 8)
                 recip(2 * (x // 8))
                 recip(2 * (x // 8) + 1)
             if 0 <= g < NG and in_psum(g):
                 scale_max(g)
-            x = g + 8
-            if x >= 8 and x % 4 == 0:
+            x = g + 4
+            if x >= 4 and x % 4 == 0:
                 tqk_ev(x // 4)
             if 0 <= g < 32 and g % 8 == 2:
                 tb_ev(g // 8)
             x = g - 3
-            if x >= 0 and x % 2 == 0:
+            if x >= 0 and x % 2 == 0 and x // 2 < NG // 2 - 2:
                 evict_e(x // 2)
             x = g - 14
-            if x >= 0 and x % 8 == 0:
+            if x >= 0 and x % 8 == 0 and x // 8 < LAST:
                 finish(2 * (x // 8))
             x = g - 18
-            if x >= 0 and x % 8 == 0:
+            if x >= 0 and x % 8 == 0 and x // 8 < LAST:
                 finish(2 * (x // 8) + 1)
             expo(g)
             x = g - 3
-            if x >= 0 and x % 2 == 0:
+            if x >= 0 and x % 2 == 0 and x // 2 < NG // 2 - 2:
                 regroup(x // 2)
+            if g == 4:
+                vregroup(0)
+            if g == 6:
+                vregroup(1)
             x = g - 11
             if x >= 0 and x % 8 == 0:
                 vregroup(x // 8 + 2)
+            if g == NG - 2:
+                vquant(LAST)
+                quant_window(NWIN - 2)
+                recip(NWIN - 2)
+            if g == NG - 1:
+                evict_direct(NG // 2 - 2)
+            if g == NG:
+                mx(NWIN - 2, spare_bank=True)
+                evict_direct(NG // 2 - 1)
+                recip(NWIN - 1)
+                quant_window(NWIN - 1)
+            if g == NG + 2:
+                finish(NWIN - 2)
+                mx(NWIN - 1)
+                finish(NWIN - 1, on_vector=True)

@@ -33,7 +33,7 @@ def tile_single_head_split_window_attention_1d_t_kernel(tc, q, k, v, attn_mask, 
     nc = tc.nc
     qv = q.flatten_outer_dims().rearrange("(r t p) c -> r p t c", t=TPR, p=P)
     kv = k.flatten_outer_dims().rearrange("(r t p) c -> r p t c", t=TPR, p=P)
-    vv = v.flatten_outer_dims().rearrange("(r t p) c -> r p t c", t=TPR, p=P)
+    vv = v.flatten_outer_dims().rearrange("(r h p e) c -> r p h (e c)", h=16, p=P, e=2)
     ov = out.flatten_outer_dims().rearrange("(r t p) c -> r p t c", t=TPR, p=P)
 
     with ExitStack() as ctx:
@@ -41,9 +41,9 @@ def tile_single_head_split_window_attention_1d_t_kernel(tc, q, k, v, attn_mask, 
         raw = ctx.enter_context(tc.tile_pool(name="raw", bufs=4))
         work = ctx.enter_context(tc.tile_pool(name="work", bufs=3))
         small = ctx.enter_context(tc.tile_pool(name="small", bufs=8))
-        ps_s = ctx.enter_context(tc.psum_pool(name="ps_s", bufs=3))
+        ps_s = ctx.enter_context(tc.psum_pool(name="ps_s", bufs=2))
         ps_e = ctx.enter_context(tc.psum_pool(name="ps_e", bufs=2))
-        ps_x = ctx.enter_context(tc.psum_pool(name="ps_x", bufs=1))
+        ps_x = ctx.enter_context(tc.psum_pool(name="ps_x", bufs=2))
         ps_o = ctx.enter_context(tc.psum_pool(name="ps_o", bufs=1))
         ps_t = ctx.enter_context(tc.psum_pool(name="ps_t", bufs=1))
         ctx.enter_context(tc.manual_schedule())
@@ -53,10 +53,10 @@ def tile_single_head_split_window_attention_1d_t_kernel(tc, q, k, v, attn_mask, 
         ident32 = const.tile([P, P], F32, name="ident32")
         make_identity(nc, ident32[:])
         bias = const.tile([P, WPR, 4, WIN], BF16, name="bias")
-        biasT = const.tile([P, WPR, 4, P], F32, name="biasT")
+        biasT = const.tile([P, WPR, 2, 4, P], F32, name="biasT")
 
         def in_psum(g):
-            return g >= 4 * WPR and g % 4 == 0
+            return g >= 4 * WPR and g % 2 == 0
 
         st = {}
 
@@ -93,7 +93,13 @@ def tile_single_head_split_window_attention_1d_t_kernel(tc, q, k, v, attn_mask, 
             else:
                 load_rows(q_raw, qv, row, cr, 0, 8)
                 load_rows(k_raw, kv, row, cr, 0, 8)
-            load_rows(v_raw, vv, row, cr, 0, 8)
+            h0 = 1 + 4 * cr
+            v_dst = v_raw[:].rearrange("p (h e) c -> p h (e c)", e=2)
+            if h0 + 4 <= 16:
+                nc.sync.dma_start(out=v_dst[:, 0:4, :], in_=vv[row, :, h0:h0 + 4, :])
+            else:
+                nc.sync.dma_start(out=v_dst[:, 0:3, :], in_=vv[row, :, h0:16, :])
+                nc.sync.dma_start(out=v_dst[:, 3:4, :], in_=vv[row, :, 0:1, :])
             st[("q", ch)] = q_raw
             st[("k", ch)] = k_raw
             st[("v", ch)] = v_raw
@@ -144,25 +150,26 @@ def tile_single_head_split_window_attention_1d_t_kernel(tc, q, k, v, attn_mask, 
             nc.scalar.copy(out=qkT[:], in_=tp[:])
             st[("qkT", wi)] = qkT
 
-        def tb_pe(r):
+        def tb_pe(n):
             bp = ps_t.tile([P, 2, 4, P], BF16, tag="tp")
-            for a in range(2):
+            for c in range(2):
                 for t in range(4):
-                    nc.tensor.transpose(bp[:, a, t, :], bias[:, 2 * r + a, 0, t * P:(t + 1) * P], ident[:])
-            st[("bp", r)] = bp
+                    nc.tensor.transpose(bp[:, c, t, :], bias[:, n, 2 * c, t * P:(t + 1) * P], ident[:])
+            st[("bp", n)] = bp
 
-        def tb_ev(r):
-            bp = st[("bp", r)]
-            nc.scalar.activation(
-                out=biasT[:, 2 * r:2 * r + 2, :, :].rearrange("p a t x -> p (a t x)"),
-                in_=bp[:].rearrange("p a t x -> p (a t x)"),
-                func=ACT.Copy, scale=UNSCALE,
+        def tb_ev(n):
+            bp = st[("bp", n)]
+            bstg = work.tile([P, 8 * P], BF16, tag="bstg", bufs=2)
+            nc.scalar.copy(out=bstg[:], in_=bp[:].rearrange("p c t x -> p (c t x)"))
+            nc.gpsimd.tensor_scalar(
+                out=biasT[:, n, :, :, :].rearrange("p c t x -> p (c t x)"), in0=bstg[:],
+                scalar1=UNSCALE, scalar2=0.0, op0=ALU.mult, op1=ALU.add,
             )
 
         def qk(g):
             wi, j = g // 4, g % 4
             qkT = st[("qkT", wi)]
-            if in_psum(g):
+            if g % 2 == 0:
                 s_ps = ps_x.tile([P, WIN], F32, tag="sx")
             else:
                 s_ps = ps_s.tile([P, WIN], F32, tag="s_ps")
@@ -177,7 +184,7 @@ def tile_single_head_split_window_attention_1d_t_kernel(tc, q, k, v, attn_mask, 
                 for t in range(4):
                     nc.tensor.matmul(
                         s_ps[:, t * P:(t + 1) * P],
-                        lhsT=biasT[:, wi % WPR, t, :],
+                        lhsT=biasT[:, wi % WPR, j // 2, t, :],
                         rhs=ident32[:],
                         start=False,
                         stop=(t == 3),
@@ -207,7 +214,9 @@ def tile_single_head_split_window_attention_1d_t_kernel(tc, q, k, v, attn_mask, 
 
         def scale_max(g):
             nmx = small.tile([P, 1], F32, tag="nmx")
-            nc.scalar.mul(out=nmx[:], in_=st[("mx_t", g)][:], mul=-SCALE)
+            nc.gpsimd.tensor_scalar(
+                out=nmx[:], in0=st[("mx_t", g)][:], scalar1=-SCALE, scalar2=0.0, op0=ALU.mult, op1=ALU.add,
+            )
             st[("nm", g)] = nmx
 
         def expo(g):
@@ -219,7 +228,7 @@ def tile_single_head_split_window_attention_1d_t_kernel(tc, q, k, v, attn_mask, 
                 st[("rs", wi)] = rs_new
             rs = st[("rs", wi)]
             nm = st[("nm", g)]
-            e = work.tile([P, WIN], BF16, tag="e", bufs=4)
+            e = work.tile([P, WIN], BF16, tag="e", bufs=5)
             if in_psum(g):
                 nc.scalar.activation(
                     out=e[:], in_=st[("s_ps", g)][:], func=ACT.Exp, bias=nm[:, 0:1], scale=SCALE,
@@ -237,75 +246,41 @@ def tile_single_head_split_window_attention_1d_t_kernel(tc, q, k, v, attn_mask, 
                 return
             pr, a = g // 2, g % 2
             if a == 0:
-                et_new = ps_e.tile([P, 2, 4, P], BF16, tag="et")
+                et_new = ps_e.tile([P, 2, 2, P], F32, tag="et")
                 st[("et", pr)] = et_new
             et = st[("et", pr)]
             e = st[("e", g)]
-            for t in range(4):
-                nc.tensor.transpose(et[:, a, t, :], e[:, t * P:(t + 1) * P], ident[:])
+            for u in range(2):
+                nc.tensor.transpose(et[:, a, u, :], e[:].bitcast(F32)[:, u * P:(u + 1) * P], ident32[:])
 
-        def evict_e(pr):
-            if pr < 0 or pr >= NG // 2:
-                return
+        def evict_e(pr, on_vector=False):
+            wi, hh = pr // 2, pr % 2
+            if hh == 0:
+                grp_new = work.tile([P, WIN, 4], BF16, tag="grp", bufs=3, align_bytes=64)
+                st[("grp", wi)] = grp_new
+            grp = st[("grp", wi)]
             et = st[("et", pr)]
-            ets = work.tile([P, 2, 4, P], BF16, tag="ets")
-            nc.scalar.copy(out=ets[:], in_=et[:])
-            st[("ets", pr)] = ets
+            dst = grp[:].rearrange("p x t -> p (x t)").bitcast(F32)[:, 512 * hh:512 * (hh + 1)].rearrange("p (a x u) -> p a x u", a=2, u=2)
+            src = et[:].rearrange("p a u x -> p a x u")
+            if on_vector:
+                nc.vector.tensor_copy(out=dst, in_=src)
+            else:
+                nc.scalar.copy(out=dst, in_=src)
 
-        def regroup(pr):
-            if pr < 0 or pr >= NG // 2:
-                return
-            ch, pos = pr // 4, pr % 4
-            if pos == 0:
-                grp_new = work.tile([P, 2 * WIN, 4], BF16, tag="grp", bufs=1, align_bytes=64)
-                st[("grp", ch)] = grp_new
-            grp = st[("grp", ch)]
-            ets = st[("ets", pr)]
-            nc.gpsimd.tensor_scalar(
-                out=grp[:, 256 * pos:256 * (pos + 1), :].rearrange("p (a x) t -> p a x t", a=2),
-                in0=ets[:].rearrange("p a t x -> p a x t"),
-                scalar1=1.0, scalar2=0.0, op0=ALU.mult, op1=ALU.add,
-            )
-
-        def evict_direct(pr):
-            ch, pos = pr // 4, pr % 4
-            grp = st[("grp", ch)]
-            et = st[("et", pr)]
-            nc.vector.tensor_copy(
-                out=grp[:, 256 * pos:256 * (pos + 1), :].rearrange("p (a x) t -> p a x t", a=2),
-                in_=et[:].rearrange("p a t x -> p a x t"),
-            )
-
-        def quant_window(wi):
-            ch, a = wi // 2, wi % 2
-            grp = st[("grp", ch)]
-            if a == 0:
-                ec_new = work.tile([P, 2 * WIN], U32, tag="ec", bufs=2, align_bytes=64)
-                es_new = work.tile([P, 2 * WIN], U8, tag="es", bufs=2, align_bytes=64)
-                st[("ec", ch)] = ec_new
-                st[("es", ch)] = es_new
-            nc.vector.quantize_mx(
-                out=st[("ec", ch)][:, a * WIN:(a + 1) * WIN].bitcast(FP8X4),
-                scales=st[("es", ch)][:, a * WIN:(a + 1) * WIN],
-                in_=grp[:, a * WIN:(a + 1) * WIN, :].rearrange("p x t -> p (x t)"),
-            )
-
-        def quant(ch):
-            if ch < 0 or ch >= NCH:
-                return
-            grp = st[("grp", ch)]
-            ec = work.tile([P, 2 * WIN], U32, tag="ec", bufs=2, align_bytes=64)
-            es = work.tile([P, 2 * WIN], U8, tag="es", bufs=2, align_bytes=64)
+        def quant(wi):
+            grp = st[("grp", wi)]
+            ec = work.tile([P, WIN], U32, tag="ec", bufs=3, align_bytes=64)
+            es = work.tile([P, WIN], U8, tag="es", bufs=3, align_bytes=64)
             nc.vector.quantize_mx(
                 out=ec[:].bitcast(FP8X4), scales=es[:], in_=grp[:].rearrange("p x t -> p (x t)"),
             )
-            st[("ec", ch)] = ec
-            st[("es", ch)] = es
+            st[("ec", wi)] = ec
+            st[("es", wi)] = es
 
         def mx(wi, spare_bank=False):
             ch, a = wi // 2, wi % 2
-            ec = st[("ec", ch)]
-            es = st[("es", ch)]
+            ec = st[("ec", wi)]
+            es = st[("es", wi)]
             vc = st[("vc", ch)]
             vs = st[("vs", ch)]
             if spare_bank:
@@ -315,8 +290,8 @@ def tile_single_head_split_window_attention_1d_t_kernel(tc, q, k, v, attn_mask, 
             for j in range(4):
                 nc.tensor.matmul_mx(
                     out=o_ps[:, j, :],
-                    lhsT=ec[:, (4 * a + j) * P:(4 * a + j + 1) * P].bitcast(FP8X4),
-                    lhsT_scale=es[:, (4 * a + j) * P:(4 * a + j + 1) * P],
+                    lhsT=ec[:, j * P:(j + 1) * P].bitcast(FP8X4),
+                    lhsT_scale=es[:, j * P:(j + 1) * P],
                     rhs=vc[:, a * C:(a + 1) * C].bitcast(FP8X4),
                     rhs_scale=vs[:, a * C:(a + 1) * C],
                     start=True,
@@ -351,20 +326,26 @@ def tile_single_head_split_window_attention_1d_t_kernel(tc, q, k, v, attn_mask, 
                 nc.sync.dma_start(out=ov[row, :, t0:TPR, :], in_=o_sb[:, 0:2, :])
                 nc.sync.dma_start(out=ov[row, :, 0:2, :], in_=o_sb[:, 2:4, :])
 
-        LAST = NCH - 1
+        def out_on_vector(wi):
+            return wi >= WPR and wi % 2 == 1
+
+        def pair_on_vector(pr):
+            return pr >= NG // 2 - 2
+
         load_chunk(0)
         load_chunk(1)
         load_chunk(2)
         tqk_pe(0)
         tqk_ev(0)
-        for g in range(-4, NG + 20):
+        for g in range(-4, NG + 8):
             if g >= 0 and g % 8 == 0:
                 load_chunk(g // 8 + 3)
             x = g + 5
             if x >= 4 and x % 4 == 0:
                 tqk_pe(x // 4)
-            if 0 <= g < 32 and g % 8 == 1:
-                tb_pe(g // 8)
+            x = g - 9
+            if 0 <= x < 4 * WPR and x % 4 == 0:
+                tb_pe(x // 4)
             x = g + 3
             if 0 <= x < NG and not in_psum(x):
                 qk(x)
@@ -372,63 +353,50 @@ def tile_single_head_split_window_attention_1d_t_kernel(tc, q, k, v, attn_mask, 
             if 0 <= x < NG and in_psum(x):
                 qk(x)
             tr_e(g - 1)
-            x = g - 12
-            if x >= 0 and x % 8 == 0 and x // 8 < LAST:
-                mx(2 * (x // 8))
-            x = g - 16
-            if x >= 0 and x % 8 == 0 and x // 8 < LAST:
-                mx(2 * (x // 8) + 1)
+            x = g - 9
+            if 0 <= x < NG and x % 4 == 0:
+                mx(x // 4, spare_bank=(x // 4 == NWIN - 1))
+            x = g + 1
+            if 0 <= x < NG and in_psum(x):
+                row_max(x)
             x = g + 2
             if 0 <= x < NG and not in_psum(x):
                 add_bias(x)
             x = g + 1
-            if 0 <= x < NG:
+            if 0 <= x < NG and not in_psum(x):
                 row_max(x)
-            x = g - 11
-            if x >= 0 and x % 8 == 0 and x // 8 < LAST:
-                vquant(x // 8)
-                quant(x // 8)
-                recip(2 * (x // 8))
-                recip(2 * (x // 8) + 1)
-            if 0 <= g < NG and in_psum(g):
-                scale_max(g)
+            x = g - 3
+            if 0 <= x < NG and x % 2 == 0 and pair_on_vector(x // 2):
+                evict_e(x // 2, on_vector=True)
+            x = g - 8
+            if 0 <= x < NG and x % 4 == 0:
+                quant(x // 4)
+                if x % 8 == 0:
+                    vquant(x // 8)
+                recip(x // 4)
+            x = g - 10
+            if 0 <= x < NG and x % 4 == 0 and out_on_vector(x // 4):
+                finish(x // 4, on_vector=True)
+            x = g + 1
+            if 0 <= x < NG and in_psum(x):
+                scale_max(x)
             x = g + 4
             if x >= 4 and x % 4 == 0:
                 tqk_ev(x // 4)
-            if 0 <= g < 32 and g % 8 == 2:
-                tb_ev(g // 8)
+            x = g - 10
+            if 0 <= x < 4 * WPR and x % 4 == 0:
+                tb_ev(x // 4)
             x = g - 3
-            if x >= 0 and x % 2 == 0 and x // 2 < NG // 2 - 2:
+            if 0 <= x < NG and x % 2 == 0 and not pair_on_vector(x // 2):
                 evict_e(x // 2)
-            x = g - 14
-            if x >= 0 and x % 8 == 0 and x // 8 < LAST:
-                finish(2 * (x // 8))
-            x = g - 18
-            if x >= 0 and x % 8 == 0 and x // 8 < LAST:
-                finish(2 * (x // 8) + 1)
+            x = g - 10
+            if 0 <= x < NG and x % 4 == 0 and not out_on_vector(x // 4):
+                finish(x // 4)
             expo(g)
-            x = g - 3
-            if x >= 0 and x % 2 == 0 and x // 2 < NG // 2 - 2:
-                regroup(x // 2)
             if g == 4:
                 vregroup(0)
             if g == 6:
                 vregroup(1)
-            x = g - 11
+            x = g - 9
             if x >= 0 and x % 8 == 0:
                 vregroup(x // 8 + 2)
-            if g == NG - 2:
-                vquant(LAST)
-                quant_window(NWIN - 2)
-                recip(NWIN - 2)
-            if g == NG - 1:
-                evict_direct(NG // 2 - 2)
-            if g == NG:
-                mx(NWIN - 2, spare_bank=True)
-                evict_direct(NG // 2 - 1)
-                recip(NWIN - 1)
-                quant_window(NWIN - 1)
-            if g == NG + 2:
-                finish(NWIN - 2)
-                mx(NWIN - 1)
-                finish(NWIN - 1, on_vector=True)

@@ -214,8 +214,8 @@ def tile_single_head_split_window_attention_1d_t_kernel(tc, q, k, v, attn_mask, 
 
         def scale_max(g):
             nmx = small.tile([P, 1], F32, tag="nmx")
-            nc.gpsimd.tensor_scalar(
-                out=nmx[:], in0=st[("mx_t", g)][:], scalar1=-SCALE, scalar2=0.0, op0=ALU.mult, op1=ALU.add,
+            nc.vector.tensor_scalar(
+                out=nmx[:], in0=st[("mx_t", g)][:], scalar1=-SCALE, scalar2=None, op0=ALU.mult,
             )
             st[("nm", g)] = nmx
 

import math
from contextlib import ExitStack

import concourse.bass as bass
import concourse.mybir as mybir
import concourse.tile as tile
from concourse.masks import make_identity

F32 = mybir.dt.float32
BF16 = mybir.dt.bfloat16
U32 = mybir.dt.uint32
U8 = mybir.dt.uint8
FP8X4 = mybir.dt.float8_e4m3fn_x4
ALU = mybir.AluOpType
ACT = mybir.ActivationFunctionType
AX = mybir.AxisListType

P = 128
C = 128
ROWS = 4
WPR = 8
WIN = 512
TPR = 32
NWIN = ROWS * WPR
NG = NWIN * 4
NCH = NWIN // 2
SCALE = 1.0 / math.sqrt(128.0)
UNSCALE = math.sqrt(128.0)
FLOPS = 2 * NWIN * 2 * WIN * WIN * C


def tile_single_head_split_window_attention_1d_t_kernel(tc, q, k, v, attn_mask, h, w, num_splits, out):
    nc = tc.nc
    qv = q.flatten_outer_dims().rearrange("(r t p) c -> r p t c", t=TPR, p=P)
    kv = k.flatten_outer_dims().rearrange("(r t p) c -> r p t c", t=TPR, p=P)
    vv = v.flatten_outer_dims().rearrange("(r h p e) c -> r p h (e c)", h=16, p=P, e=2)
    ov = out.flatten_outer_dims().rearrange("(r t p) c -> r p t c", t=TPR, p=P)

    with ExitStack() as ctx:
        const = ctx.enter_context(tc.tile_pool(name="const", bufs=1))
        raw = ctx.enter_context(tc.tile_pool(name="raw", bufs=4))
        work = ctx.enter_context(tc.tile_pool(name="work", bufs=3))
        small = ctx.enter_context(tc.tile_pool(name="small", bufs=8))
        ps_s = ctx.enter_context(tc.psum_pool(name="ps_s", bufs=2))
        ps_e = ctx.enter_context(tc.psum_pool(name="ps_e", bufs=2))
        ps_x = ctx.enter_context(tc.psum_pool(name="ps_x", bufs=2))
        ps_o = ctx.enter_context(tc.psum_pool(name="ps_o", bufs=1))
        ps_t = ctx.enter_context(tc.psum_pool(name="ps_t", bufs=1))
        ctx.enter_context(tc.manual_schedule())

        ident = const.tile([P, P], BF16, name="ident")
        make_identity(nc, ident[:])
        ident32 = const.tile([P, P], F32, name="ident32")
        make_identity(nc, ident32[:])
        bias = const.tile([P, WPR, 4, WIN], BF16, name="bias")
        biasT = const.tile([P, WPR, 2, 4, P], F32, name="biasT")

        def in_psum(g):
            return g >= 4 * WPR and g % 2 == 0

        st = {}

        def load_rows(dst, src, row, ch_in_row, lo, hi):
            t0 = 2 + 8 * ch_in_row
            cut = min(max(TPR - t0, lo), hi)
            if cut > lo:
                nc.sync.dma_start(out=dst[:, lo:cut, :], in_=src[row, :, t0 + lo:t0 + cut, :])
            if hi > cut:
                nc.sync.dma_start(out=dst[:, cut:hi, :], in_=src[row, :, t0 + cut - TPR:t0 + hi - TPR, :])

        def load_bias(n, lo, hi):
            nc.sync.dma_start(
                out=bias[:, n, lo:hi, :],
                in_=attn_mask[n, lo * P:hi * P, :].rearrange("(j p) x -> p j x", p=P),
            )

        def load_chunk(ch):
            if ch >= NCH:
                return
            row, cr = ch // 4, ch % 4
            q_raw = raw.tile([P, 8, C], BF16, tag="q_raw")
            k_raw = raw.tile([P, 8, C], BF16, tag="k_raw")
            v_raw = raw.tile([P, 8, C], BF16, tag="v_raw")
            if row == 0:
                for a in range(2):
                    load_rows(q_raw, qv, row, cr, 4 * a, 4 * a + 4)
                    load_rows(k_raw, kv, row, cr, 4 * a, 4 * a + 4)
                    if ch == 0 and a == 0:
                        load_bias(0, 0, 1)
                        load_bias(0, 1, 4)
                    else:
                        load_bias(2 * cr + a, 0, 4)
            else:
                load_rows(q_raw, qv, row, cr, 0, 8)
                load_rows(k_raw, kv, row, cr, 0, 8)
            h0 = 1 + 4 * cr
            v_dst = v_raw[:].rearrange("p (h e) c -> p h (e c)", e=2)
            if h0 + 4 <= 16:
                nc.sync.dma_start(out=v_dst[:, 0:4, :], in_=vv[row, :, h0:h0 + 4, :])
            else:
                nc.sync.dma_start(out=v_dst[:, 0:3, :], in_=vv[row, :, h0:16, :])
                nc.sync.dma_start(out=v_dst[:, 3:4, :], in_=vv[row, :, 0:1, :])
            st[("q", ch)] = q_raw
            st[("k", ch)] = k_raw
            st[("v", ch)] = v_raw

        def vregroup(ch):
            if ch >= NCH:
                return
            v_raw = st[("v", ch)]
            vg = work.tile([P, 2, C, 4], BF16, tag="vg", bufs=2, align_bytes=64)
            nc.gpsimd.tensor_scalar(
                out=vg[:], in0=v_raw[:].rearrange("p (a t) c -> p a c t", a=2),
                scalar1=1.0, scalar2=0.0, op0=ALU.mult, op1=ALU.add,
            )
            st[("vg", ch)] = vg

        def vquant(ch):
            if ch >= NCH:
                return
            vg = st[("vg", ch)]
            vc = work.tile([P, 2 * C], U32, tag="vc", align_bytes=64)
            vs = work.tile([P, 2 * C], U8, tag="vs", align_bytes=64)
            nc.vector.quantize_mx(
                out=vc[:].bitcast(FP8X4),
                scales=vs[:],
                in_=vg[:].rearrange("p a c t -> p (a c t)"),
            )
            st[("vc", ch)] = vc
            st[("vs", ch)] = vs

        def tqk_pe(wi):
            if wi >= NWIN:
                return
            ch, a = wi // 2, wi % 2
            q_raw = st[("q", ch)]
            k_raw = st[("k", ch)]
            tp = ps_t.tile([P, 8, P], BF16, tag="tp")
            for j in range(4):
                nc.tensor.transpose(tp[:, j, :], q_raw[:, 4 * a + j, :], ident[:])
            for j in range(4):
                nc.tensor.transpose(tp[:, 4 + j, :], k_raw[:, 4 * a + j, :], ident[:])
            st[("tp", wi)] = tp

        def tqk_ev(wi):
            if wi >= NWIN:
                return
            tp = st[("tp", wi)]
            qkT = work.tile([P, 8, P], BF16, tag="qkT", bufs=4)
            nc.scalar.copy(out=qkT[:], in_=tp[:])
            st[("qkT", wi)] = qkT

        def tb_pe(n):
            bp = ps_t.tile([P, 2, 4, P], BF16, tag="tp")
            for c in range(2):
                for t in range(4):
                    nc.tensor.transpose(bp[:, c, t, :], bias[:, n, 2 * c, t * P:(t + 1) * P], ident[:])
            st[("bp", n)] = bp

        def tb_ev(n):
            bp = st[("bp", n)]
            bstg = work.tile([P, 8 * P], BF16, tag="bstg", bufs=2)
            nc.scalar.copy(out=bstg[:], in_=bp[:].rearrange("p c t x -> p (c t x)"))
            nc.gpsimd.tensor_scalar(
                out=biasT[:, n, :, :, :].rearrange("p c t x -> p (c t x)"), in0=bstg[:],
                scalar1=UNSCALE, scalar2=0.0, op0=ALU.mult, op1=ALU.add,
            )

        def qk(g):
            wi, j = g // 4, g % 4
            qkT = st[("qkT", wi)]
            if g % 2 == 0:
                s_ps = ps_x.tile([P, WIN], F32, tag="sx")
            else:
                s_ps = ps_s.tile([P, WIN], F32, tag="s_ps")
            nc.tensor.matmul(
                s_ps[:],
                lhsT=qkT[:, j, :],
                rhs=qkT[:, 4:8, :].rearrange("c t x -> c (t x)"),
                start=True,
                stop=not in_psum(g),
            )
            if in_psum(g):
                for t in range(4):
                    nc.tensor.matmul(
                        s_ps[:, t * P:(t + 1) * P],
                        lhsT=biasT[:, wi % WPR, j // 2, t, :],
                        rhs=ident32[:],
                        start=False,
                        stop=(t == 3),
                        is_transpose=True,
                    )
            st[("s_ps", g)] = s_ps

        def add_bias(g):
            wi, j = g // 4, g % 4
            s_ps = st[("s_ps", g)]
            ns = work.tile([P, WIN], F32, tag="ns", bufs=4)
            nc.vector.scalar_tensor_tensor(
                out=ns[:], in0=s_ps[:], scalar=-SCALE, in1=bias[:, wi % WPR, j, :],
                op0=ALU.mult, op1=ALU.subtract,
            )
            st[("ns", g)] = ns

        def row_max(g):
            if in_psum(g):
                mx_t = small.tile([P, 1], F32, tag="mx_t")
                nc.vector.tensor_reduce(out=mx_t[:], in_=st[("s_ps", g)][:], axis=AX.X, op=ALU.max)
                st[("mx_t", g)] = mx_t
            else:
                nm = small.tile([P, 1], F32, tag="nm")
                nc.vector.tensor_reduce(out=nm[:], in_=st[("ns", g)][:], axis=AX.X, op=ALU.min)
                st[("nm", g)] = nm

        def scale_max(g):
            nmx = small.tile([P, 1], F32, tag="nmx")
            nc.vector.tensor_scalar(
                out=nmx[:], in0=st[("mx_t", g)][:], scalar1=-SCALE, scalar2=None, op0=ALU.mult,
            )
            st[("nm", g)] = nmx

        def expo(g):
            if g < 0 or g >= NG:
                return
            wi, j = g // 4, g % 4
            if j == 0:
                rs_new = small.tile([P, 4], F32, tag="rs")
                st[("rs", wi)] = rs_new
            rs = st[("rs", wi)]
            nm = st[("nm", g)]
            e = work.tile([P, WIN], BF16, tag="e", bufs=5)
            if in_psum(g):
                nc.scalar.activation(
                    out=e[:], in_=st[("s_ps", g)][:], func=ACT.Exp, bias=nm[:, 0:1], scale=SCALE,
                    accum_out=rs[:, j:j + 1],
                )
            else:
                nc.scalar.activation(
                    out=e[:], in_=st[("ns", g)][:], func=ACT.Exp, bias=nm[:, 0:1], scale=-1.0,
                    accum_out=rs[:, j:j + 1],
                )
            st[("e", g)] = e

        def tr_e(g):
            if g < 0 or g >= NG:
                return
            pr, a = g // 2, g % 2
            if a == 0:
                et_new = ps_e.tile([P, 2, 2, P], F32, tag="et")
                st[("et", pr)] = et_new
            et = st[("et", pr)]
            e = st[("e", g)]
            for u in range(2):
                nc.tensor.transpose(et[:, a, u, :], e[:].bitcast(F32)[:, u * P:(u + 1) * P], ident32[:])

        def evict_e(pr, on_vector=False):
            wi, hh = pr // 2, pr % 2
            if hh == 0:
                grp_new = work.tile([P, WIN, 4], BF16, tag="grp", bufs=3, align_bytes=64)
                st[("grp", wi)] = grp_new
            grp = st[("grp", wi)]
            et = st[("et", pr)]
            dst = grp[:].rearrange("p x t -> p (x t)").bitcast(F32)[:, 512 * hh:512 * (hh + 1)].rearrange("p (a x u) -> p a x u", a=2, u=2)
            src = et[:].rearrange("p a u x -> p a x u")
            if on_vector:
                nc.vector.tensor_copy(out=dst, in_=src)
            else:
                nc.scalar.copy(out=dst, in_=src)

        def quant(wi):
            grp = st[("grp", wi)]
            ec = work.tile([P, WIN], U32, tag="ec", bufs=3, align_bytes=64)
            es = work.tile([P, WIN], U8, tag="es", bufs=3, align_bytes=64)
            nc.vector.quantize_mx(
                out=ec[:].bitcast(FP8X4), scales=es[:], in_=grp[:].rearrange("p x t -> p (x t)"),
            )
            st[("ec", wi)] = ec
            st[("es", wi)] = es

        def mx(wi, spare_bank=False):
            ch, a = wi // 2, wi % 2
            ec = st[("ec", wi)]
            es = st[("es", wi)]
            vc = st[("vc", ch)]
            vs = st[("vs", ch)]
            if spare_bank:
                o_ps = ps_x.tile([P, 4, C], F32, tag="sx")
            else:
                o_ps = ps_o.tile([P, 4, C], F32, tag="o_ps")
            for j in range(4):
                nc.tensor.matmul_mx(
                    out=o_ps[:, j, :],
                    lhsT=ec[:, j * P:(j + 1) * P].bitcast(FP8X4),
                    lhsT_scale=es[:, j * P:(j + 1) * P],
                    rhs=vc[:, a * C:(a + 1) * C].bitcast(FP8X4),
                    rhs_scale=vs[:, a * C:(a + 1) * C],
                    start=True,
                    stop=True,
                )
            st[("o_ps", wi)] = o_ps

        def recip(wi):
            if wi < 0 or wi >= NWIN:
                return
            rs = st[("rs", wi)]
            ri = small.tile([P, 4], F32, tag="ri")
            nc.vector.reciprocal(out=ri[:], in_=rs[:])
            st[("ri", wi)] = ri

        def finish(wi, on_vector=False):
            row, n = wi // WPR, wi % WPR
            o_ps = st[("o_ps", wi)]
            ri = st[("ri", wi)]
            o_sb = work.tile([P, 4, C], F32, tag="o_sb")
            if on_vector:
                nc.vector.tensor_tensor(
                    out=o_sb[:], in0=o_ps[:], in1=ri[:].unsqueeze(2).to_broadcast([P, 4, C]), op=ALU.mult,
                )
            else:
                for j in range(4):
                    nc.scalar.activation(out=o_sb[:, j, :], in_=o_ps[:, j, :], func=ACT.Copy, scale=ri[:, j:j + 1])
            t0 = 2 + 4 * n
            if t0 + 4 <= TPR:
                nc.sync.dma_start(out=ov[row, :, t0:t0 + 4, :], in_=o_sb[:])
            else:
                nc.sync.dma_start(out=ov[row, :, t0:TPR, :], in_=o_sb[:, 0:2, :])
                nc.sync.dma_start(out=ov[row, :, 0:2, :], in_=o_sb[:, 2:4, :])

        def out_on_vector(wi):
            return wi >= WPR and wi % 2 == 1

        def pair_on_vector(pr):
            return pr >= NG // 2 - 2

        load_chunk(0)
        load_chunk(1)
        load_chunk(2)
        tqk_pe(0)
        tqk_ev(0)
        for g in range(-4, NG + 8):
            if g >= 0 and g % 8 == 0:
                load_chunk(g // 8 + 3)
            x = g + 5
            if x >= 4 and x % 4 == 0:
                tqk_pe(x // 4)
            x = g - 9
            if 0 <= x < 4 * WPR and x % 4 == 0:
                tb_pe(x // 4)
            x = g + 3
            if 0 <= x < NG and not in_psum(x):
                qk(x)
            x = g + 2
            if 0 <= x < NG and in_psum(x):
                qk(x)
            tr_e(g - 1)
            x = g - 9
            if 0 <= x < NG and x % 4 == 0:
                mx(x // 4, spare_bank=(x // 4 == NWIN - 1))
            x = g + 1
            if 0 <= x < NG and in_psum(x):
                row_max(x)
            x = g + 2
            if 0 <= x < NG and not in_psum(x):
                add_bias(x)
            x = g + 1
            if 0 <= x < NG and not in_psum(x):
                row_max(x)
            x = g - 3
            if 0 <= x < NG and x % 2 == 0 and pair_on_vector(x // 2):
                evict_e(x // 2, on_vector=True)
            x = g - 8
            if 0 <= x < NG and x % 4 == 0:
                quant(x // 4)
                if x % 8 == 0:
                    vquant(x // 8)
                recip(x // 4)
            x = g - 10
            if 0 <= x < NG and x % 4 == 0 and out_on_vector(x // 4):
                finish(x // 4, on_vector=True)
            x = g + 1
            if 0 <= x < NG and in_psum(x):
                scale_max(x)
            x = g + 4
            if x >= 4 and x % 4 == 0:
                tqk_ev(x // 4)
            x = g - 10
            if 0 <= x < 4 * WPR and x % 4 == 0:
                tb_ev(x // 4)
            x = g - 3
            if 0 <= x < NG and x % 2 == 0 and not pair_on_vector(x // 2):
                evict_e(x // 2)
            x = g - 10
            if 0 <= x < NG and x % 4 == 0 and not out_on_vector(x // 4):
                finish(x // 4)
            expo(g)
            if g == 4:
                vregroup(0)
            if g == 6:
                vregroup(1)
            x = g - 9
            if x >= 0 and x % 8 == 0:
                vregroup(x // 8 + 2)
